import numpy as np
import ml_dtypes


def mxq(x, axis, fmt="e4m3"):
    dtype, down = {"e4m3": (ml_dtypes.float8_e4m3fn, 7), "e5m2": (ml_dtypes.float8_e5m2, 14)}[fmt]
    v = np.moveaxis(np.asarray(x, np.float32).astype(ml_dtypes.bfloat16).astype(np.float64), axis, -1)
    blocks = v.reshape(v.shape[:-1] + (-1, 32))
    amax = np.abs(blocks).max(-1, keepdims=True)
    byte = np.maximum(np.where(amax > 0, np.frexp(amax)[1] - 1 + 127, 0) - down, 1)
    scale = np.exp2(byte - 127.0)
    codes = (blocks / scale).astype(np.float32).astype(dtype).astype(np.float64)
    return np.moveaxis((codes * scale).reshape(v.shape), -1, axis)


WIDE = False


def mx_kscale(k):
    if not WIDE:
        return np.ones(k)
    levels = np.array([10, -10, 5, -5, 0])
    if k % 512:
        return np.exp2(np.random.permutation(np.resize(levels, k // 32))).repeat(32)
    a = np.empty((k // 512, 16))
    for p in range(k // 512):
        a[p, :8] = np.random.permutation(np.resize(levels, 8))
        for g in range(8):
            far = levels[np.abs(levels - a[p, g]) >= 10]
            a[p, g + 8] = far[np.random.randint(len(far))]
    return np.exp2(a.ravel()).repeat(32)


BF16 = ml_dtypes.bfloat16


def bf(x):
    return np.asarray(x, np.float32).astype(BF16)


def f64(x):
    return np.asarray(x).astype(np.float64)


B, L, D, E, S = 8, 1024, 1024, 64, 128
F = E + E + S
LN_EPS = 1e-5
GQ = 1.75 * np.sqrt(np.sqrt(10.0 * L / S))


def silu(v):
    return v / (1.0 + np.exp(-v))


def setup_inputs():
    n = np.random.standard_normal
    s = mx_kscale(D)
    return {"x": bf(0.7 * n((B, L, D)) + 0.3 * n((B, L, 1))),
            "ln_g": bf((1.0 + 0.1 * n(D)) * s),
            "ln_b": bf(0.1 * n(D) * s),
            "W_in": bf(n((D, F)) / np.sqrt(D) / s[:, None]),
            "b_in": bf(0.2 * n(F)),
            "gamma_q": bf(GQ * (1.0 + 0.1 * n(S))),
            "beta_q": bf(GQ * (-0.2 + 0.1 * n(S))),
            "gamma_k": bf(GQ * (1.0 + 0.1 * n(S))),
            "beta_k": bf(GQ * (-0.2 + 0.1 * n(S)))}


def reference(x, ln_g, ln_b, W_in, b_in, gamma_q, beta_q, gamma_k, beta_k):
    x = f64(x)
    mu = x.mean(-1, keepdims=True)
    var = np.square(x - mu).mean(-1, keepdims=True)
    xn = (x - mu) / np.sqrt(var + LN_EPS) * f64(ln_g) + f64(ln_b)
    uvz = silu((mxq(xn, 2, "e4m3") @ mxq(f64(W_in), 0, "e4m3")) + f64(b_in))
    u, v, z = uvz[..., :E], uvz[..., E:E + E], uvz[..., E + E:]
    q = z * f64(gamma_q) + f64(beta_q)
    k = z * f64(gamma_k) + f64(beta_k)
    return u, v, q, k

@@ -1,0 +1,336 @@
+from contextlib import ExitStack
+
+import concourse.mybir as mybir
+from concourse.masks import make_identity
+
+F32 = mybir.dt.float32
+BF16 = mybir.dt.bfloat16
+U32 = mybir.dt.uint32
+U8 = mybir.dt.uint8
+FP8X4 = mybir.dt.float8_e4m3fn_x4
+ACT = mybir.ActivationFunctionType
+ALU = mybir.AluOpType
+
+P = 128
+ROWS = 8 * 1024
+D = 1024
+F = 256
+E = 64
+S = 128
+LN_EPS = 1e-5
+PACK = 4
+K_PASS = P * PACK
+PASSES = D // K_PASS
+K_BLOCKS = D // P
+TILES = 4
+GROUP = TILES * P
+GROUPS = ROWS // GROUP
+BN_MAX = 512
+FLOPS = 2 * ROWS * D * F
+
+LOAD_AHEAD = 4
+STAT_AHEAD = 3
+XHAT_AHEAD = 2
+assert XHAT_AHEAD == STAT_AHEAD - 1
+
+XHAT_SHARES = (
+    ("gpsimd", 0, 0, D),
+    ("gpsimd", 1, 0, D),
+    ("vector", 2, 0, D // 2),
+    ("scalar", 2, D // 2, D),
+    ("scalar", 3, 0, D),
+)
+XHAT_SHARES_OF_LAST = (("vector", 0, 0, D), ("vector", 1, 0, D), ("vector", 2, 0, D), ("vector", 3, 0, D))
+
+COL_BIAS = 0
+COL_GAMMA_BETA = COL_BIAS + F // P
+PARAM_COLS = 32
+
+
+def tile_gaublock_pb_t_kernel(
+    tc, x, ln_g, ln_b, W_in, b_in, gamma_q, beta_q, gamma_k, beta_k, out_0, out_1, out_2, out_3
+):
+    nc = tc.nc
+    x_rows = x.flatten_outer_dims()
+    outs = (
+        out_0.flatten_outer_dims(),
+        out_1.flatten_outer_dims(),
+        out_2.flatten_outer_dims(),
+        out_3.flatten_outer_dims(),
+    )
+
+    with ExitStack() as ctx:
+        const = ctx.enter_context(tc.tile_pool(name="const", bufs=1))
+        x_pool = ctx.enter_context(tc.tile_pool(name="x_pool", bufs=LOAD_AHEAD + 1))
+        row_pool = ctx.enter_context(tc.tile_pool(name="row_pool", bufs=STAT_AHEAD + 2))
+        work = ctx.enter_context(tc.tile_pool(name="work", bufs=2))
+        store_pool = ctx.enter_context(tc.tile_pool(name="store_pool", bufs=3))
+        turn_banks = ctx.enter_context(tc.psum_pool(name="turn_banks", bufs=6))
+        mx_banks = ctx.enter_context(tc.psum_pool(name="mx_banks", bufs=2))
+        ctx.enter_context(tc.manual_schedule())
+
+        tiles = {}
+
+        def live(g):
+            return 0 <= g < GROUPS
+
+        def shares(g):
+            return XHAT_SHARES_OF_LAST if g == GROUPS - 1 else XHAT_SHARES
+
+        def load(g):
+            xt = x_pool.tile([P, TILES, D], BF16, name="xt")
+            tiles[("x", g)] = xt
+            src = x_rows[g * GROUP : (g + 1) * GROUP, :].rearrange("(p t) k -> p t k", t=TILES)
+            if g == 0:
+                for t in range(TILES):
+                    nc.sync.dma_start(out=xt[:, t, :], in_=src[:, t, :])
+            else:
+                nc.sync.dma_start(out=xt[:], in_=src)
+
+        load(0)
+        ident = const.tile([P, P], F32)
+        make_identity(nc, ident[:])
+        minus_half = const.tile([P, TILES], F32)
+        nc.vector.memset(minus_half[:], -0.5)
+        param_rows = const.tile([P, P], BF16)
+        nc.vector.memset(param_rows[:], 0.0)
+        row = 0
+        gain_bf16 = const.tile([P, PASSES, PACK], BF16)
+        offset_bf16 = const.tile([P, PASSES, PACK], BF16)
+        for dst, vec in ((gain_bf16, ln_g), (offset_bf16, ln_b)):
+            nc.scalar.dma_start(out=dst[:], in_=vec.rearrange("(c p t) -> p c t", p=P, t=PACK))
+        for vec in (b_in, gamma_q, beta_q, gamma_k, beta_k):
+            n = vec.shape[0] // P
+            nc.scalar.dma_start(out=param_rows[row : row + n, :], in_=vec.rearrange("(j p) -> j p", p=P))
+            row += n
+        load(1)
+        w_raw = const.tile([P, PASSES, PACK, F], BF16)
+        nc.sync.dma_start(out=w_raw[:], in_=W_in.rearrange("(c p t) f -> p c t f", p=P, t=PACK))
+        for g in range(2, LOAD_AHEAD):
+            load(g)
+
+        gain = const.tile([P, PASSES, PACK], F32)
+        offset = const.tile([P, PASSES, PACK], F32)
+        params = const.tile([P, PARAM_COLS], F32)
+        w_codes = const.tile([P, PASSES * F], U32, align_bytes=64)
+        w_scales = const.tile([P, PASSES * F], U8, align_bytes=64)
+
+        def param(col):
+            return params[:, col : col + 1]
+
+        def prepare_params():
+            nc.vector.tensor_copy(out=gain[:], in_=gain_bf16[:])
+            nc.vector.tensor_copy(out=offset[:], in_=offset_bf16[:])
+            param_f32 = const.tile([P, P], F32)
+            nc.vector.tensor_copy(out=param_f32[:], in_=param_rows[:])
+            bank = turn_banks.tile([P, GROUP], F32, tag="bank", name="param_bank")
+            nc.tensor.transpose(out=bank[:, 0:P], in_=param_f32[:], identity=ident[:])
+            nc.vector.tensor_copy(out=params[:], in_=bank[:, 0:PARAM_COLS])
+
+        def prepare_w():
+            w_words = const.tile([P, PASSES, F, PACK], BF16, align_bytes=64)
+            nc.vector.tensor_copy(out=w_words[:], in_=w_raw[:].rearrange("p c t f -> p c f t"))
+            nc.vector.quantize_mx(
+                out=w_codes[:].bitcast(FP8X4),
+                scales=w_scales[:],
+                in_=w_words[:].rearrange("p c f t -> p (c f t)"),
+            )
+
+        def stats_tile(g, t):
+            if t == 0:
+                tiles[("stats", g)] = row_pool.tile([P, TILES, D // BN_MAX, 6], F32, name="stats")
+                tiles[("mean_var", g)] = row_pool.tile([P, TILES, 2], F32, name="mean_var")
+            for h in range(D // BN_MAX):
+                nc.vector.bn_stats(
+                    out=tiles[("stats", g)][:, t, h, :], in_=tiles[("x", g)][:, t, h * BN_MAX : (h + 1) * BN_MAX]
+                )
+
+        def aggregate(g, t):
+            nc.vector.bn_aggr(
+                out=tiles[("mean_var", g)][:, t, :],
+                in_=tiles[("stats", g)][:, t, :, :].rearrange("p h s -> p (h s)"),
+            )
+
+        def row_scalars(g):
+            mean_var = tiles[("mean_var", g)]
+            neg_mean = row_pool.tile([P, TILES], F32, name="neg_mean")
+            var_eps = row_pool.tile([P, TILES], F32, name="var_eps")
+            nc.vector.tensor_scalar(out=neg_mean[:], in0=mean_var[:, :, 0], scalar1=-1.0, scalar2=None, op0=ALU.mult)
+            nc.vector.tensor_scalar(out=var_eps[:], in0=mean_var[:, :, 1], scalar1=LN_EPS, scalar2=None, op0=ALU.add)
+            tiles[("neg_mean", g)] = neg_mean
+            tiles[("var_eps", g)] = var_eps
+
+        def inverse_std(g):
+            rstd = row_pool.tile([P, TILES], F32, name="rstd")
+            nc.gpsimd.tensor_tensor(out=rstd[:], in0=tiles[("var_eps", g)][:], in1=minus_half[:], op=ALU.pow)
+            tiles[("rstd", g)] = rstd
+
+        def scalar_bias(g):
+            bias = row_pool.tile([P, TILES], F32, name="bias")
+            nc.gpsimd.tensor_tensor(
+                out=bias[:], in0=tiles[("neg_mean", g)][:], in1=tiles[("rstd", g)][:], op=ALU.mult
+            )
+            tiles[("bias", g)] = bias
+
+        def xhat(g, engine):
+            mine = [share[1:] for share in shares(g) if share[0] == engine]
+            if mine and ("xhat", g) not in tiles:
+                tiles[("xhat", g)] = work.tile([P, TILES, D], F32, name="xhat")
+            for t, lo, hi in mine:
+                dst = tiles[("xhat", g)][:, t, lo:hi].rearrange("p (c t k) -> p c t k", t=PACK, k=P)
+                src = tiles[("x", g)][:, t, lo:hi].rearrange("p (c k t) -> p c t k", t=PACK, k=P)
+                rstd = tiles[("rstd", g)][:, t : t + 1]
+                if engine == "scalar":
+                    nc.scalar.activation(
+                        out=dst, in_=src, func=ACT.Identity, bias=tiles[("bias", g)][:, t : t + 1], scale=rstd
+                    )
+                else:
+                    eng = nc.gpsimd if engine == "gpsimd" else nc.vector
+                    eng.tensor_scalar(
+                        out=dst, in0=src, scalar1=tiles[("neg_mean", g)][:, t : t + 1], scalar2=rstd,
+                        op0=ALU.add, op1=ALU.mult,
+                    )
+
+        def turn(g, j):
+            if j == 0:
+                tiles[("planes", g)] = work.tile([P, PASSES, PACK, GROUP], BF16, name="planes")
+            bank = turn_banks.tile([P, GROUP], F32, tag="bank", name="bank")
+            for t in range(TILES):
+                nc.tensor.transpose(
+                    out=bank[:, t * P : (t + 1) * P],
+                    in_=tiles[("xhat", g)][:, t, j * P : (j + 1) * P],
+                    identity=ident[:],
+                )
+            nc.scalar.activation(
+                out=tiles[("planes", g)][:, j // PACK, j % PACK, :], in_=bank[:], func=ACT.Identity,
+                bias=offset[:, j // PACK, j % PACK : j % PACK + 1], scale=gain[:, j // PACK, j % PACK : j % PACK + 1],
+            )
+
+        def regroup(g, c):
+            if c == 0:
+                tiles[("words", g)] = work.tile([P, PASSES, GROUP, PACK], BF16, align_bytes=64, name="words")
+            nc.vector.tensor_copy(
+                out=tiles[("words", g)][:, c].rearrange("p (w i) t -> p w t i", i=4),
+                in_=tiles[("planes", g)][:, c].rearrange("p t (w i) -> p w t i", i=4),
+            )
+
+        def quantise(g):
+            codes = work.tile([P, PASSES * GROUP], U32, align_bytes=64, name="codes")
+            scales = work.tile([P, PASSES * GROUP], U8, align_bytes=64, name="scales")
+            nc.vector.quantize_mx(
+                out=codes[:].bitcast(FP8X4), scales=scales[:],
+                in_=tiles[("words", g)][:].rearrange("p c n t -> p (c n t)"),
+            )
+            tiles[("codes", g)] = codes
+            tiles[("scales", g)] = scales
+
+        def multiply(g):
+            codes = tiles[("codes", g)]
+            scales = tiles[("scales", g)]
+            silu = work.tile([P, F // P, GROUP], F32, name="silu")
+            tiles[("silu", g)] = silu
+            accs = []
+            for h in range(F // P):
+                acc = mx_banks.tile([P, GROUP], F32, name="acc")
+                accs.append(acc)
+                for c in range(PASSES):
+                    w0 = c * F + h * P
+                    nc.tensor.matmul_mx(
+                        out=acc[:],
+                        lhsT=w_codes[:, w0 : w0 + P].bitcast(FP8X4),
+                        lhsT_scale=w_scales[:, w0 : w0 + P],
+                        rhs=codes[:, c * GROUP : (c + 1) * GROUP].bitcast(FP8X4),
+                        rhs_scale=scales[:, c * GROUP : (c + 1) * GROUP],
+                        start=(c == 0),
+                        stop=(c == PASSES - 1),
+                    )
+            for h in range(F // P):
+                nc.scalar.activation(
+                    out=silu[:, h, :], in_=accs[h][:], func=ACT.Silu, bias=param(COL_BIAS + h), scale=1.0
+                )
+
+        def scale_offset(g):
+            z = tiles[("silu", g)][:, 1, :]
+            qk = work.tile([P, 2, GROUP], F32, name="qk")
+            tiles[("qk", g)] = qk
+            for i in range(2):
+                nc.vector.tensor_scalar(
+                    out=qk[:, i, :], in0=z,
+                    scalar1=param(COL_GAMMA_BETA + 2 * i), scalar2=param(COL_GAMMA_BETA + 2 * i + 1),
+                    op0=ALU.mult, op1=ALU.add,
+                )
+
+        def emit_out(g, i):
+            src = tiles[("silu", g)][:, 0, :] if i == 0 else tiles[("qk", g)][:, i - 1, :]
+            rows = slice(g * GROUP, (g + 1) * GROUP)
+            bank = turn_banks.tile([P, GROUP], F32, tag="bank", name="out_bank")
+            for t in range(TILES):
+                nc.tensor.transpose(
+                    out=bank[:, t * P : (t + 1) * P], in_=src[:, t * P : (t + 1) * P], identity=ident[:]
+                )
+            if i == 0:
+                uv = store_pool.tile([P, 2, TILES, E], F32, name="uv")
+                nc.scalar.copy(
+                    out=uv[:].rearrange("p c t f -> p t c f"),
+                    in_=bank[:].rearrange("p (t c f) -> p t c f", t=TILES, c=2),
+                )
+                for c in range(2):
+                    nc.sync.dma_start(
+                        out=outs[c][rows, :].rearrange("(p t) f -> p (t f)", t=TILES),
+                        in_=uv[:, c].rearrange("p t f -> p (t f)"),
+                    )
+            else:
+                q_or_k = store_pool.tile([P, TILES * S], F32, name="q_or_k", bufs=6)
+                nc.scalar.copy(out=q_or_k[:], in_=bank[:])
+                nc.sync.dma_start(
+                    out=outs[1 + i][rows, :].rearrange("(p t) f -> p (t f)", t=TILES), in_=q_or_k[:]
+                )
+
+        for i in range(-STAT_AHEAD, GROUPS + 1):
+            g_stat = i + STAT_AHEAD
+            g_xhat = i + XHAT_AHEAD
+            if i >= 0 and live(i + LOAD_AHEAD):
+                load(i + LOAD_AHEAD)
+
+            if live(g_xhat - 1):
+                xhat(g_xhat - 1, "vector")
+            if live(i):
+                regroup(i, 0)
+            if live(g_stat - 1):
+                aggregate(g_stat - 1, TILES - 1)
+            if live(i):
+                regroup(i, 1)
+            if live(i) and not live(g_stat):
+                quantise(i)
+            if live(i - 1):
+                scale_offset(i - 1)
+            if live(g_stat - 1):
+                row_scalars(g_stat - 1)
+            if live(i) and live(g_stat):
+                quantise(i)
+
+            if live(g_xhat):
+                inverse_std(g_xhat)
+                if any(share[0] == "scalar" for share in shares(g_xhat)):
+                    scalar_bias(g_xhat)
+                xhat(g_xhat, "gpsimd")
+            if live(g_stat):
+                stats_tile(g_stat, 0)
+                for t in range(1, TILES):
+                    stats_tile(g_stat, t)
+                    aggregate(g_stat, t - 1)
+            if g_stat == 0:
+                prepare_params()
+            if g_stat == 1:
+                prepare_w()
+
+            if live(i + 1):
+                for j in range(K_BLOCKS):
+                    turn(i + 1, j)
+            if live(g_xhat):
+                xhat(g_xhat, "scalar")
+            if live(i):
+                multiply(i)
+            if live(i - 1):
+                for k in range(3):
+                    emit_out(i - 1, k)

@@ -24,7 +24,9 @@ PASSES = D // K_PASS
 K_BLOCKS = D // P
 TILES = 4
 GROUP = TILES * P
-GROUPS = ROWS // GROUP
+GROUP_TILES = (4,) * 16
+GROUPS = len(GROUP_TILES)
+assert sum(GROUP_TILES) * P == ROWS
 BN_MAX = 512
 FLOPS = 2 * ROWS * D * F
 
@@ -33,14 +35,31 @@ STAT_AHEAD = 3
 XHAT_AHEAD = 2
 assert XHAT_AHEAD == STAT_AHEAD - 1
 
-XHAT_SHARES = (
-    ("gpsimd", 0, 0, D),
-    ("gpsimd", 1, 0, D),
-    ("vector", 2, 0, D // 2),
-    ("scalar", 2, D // 2, D),
-    ("scalar", 3, 0, D),
-)
-XHAT_SHARES_OF_LAST = (("vector", 0, 0, D), ("vector", 1, 0, D), ("vector", 2, 0, D), ("vector", 3, 0, D))
+GS = 18
+VS = 0
+COPY_S = 0
+EXIT_V = ()
+WS = 1
+RUN = 4
+
+
+def share_table(n):
+    g, v = GS * n // 4, VS * n // 4
+    out = []
+    for t in range(n):
+        a, b, e = min(max(g - 8 * t, 0), 8), min(max(g + v - 8 * t, 0), 8), 8
+        for eng, lo, hi in (("gpsimd", 0, a), ("vector", a, b), ("scalar", b, e)):
+            if hi > lo:
+                if lo < 4 < hi and (lo, hi) != (0, 8):
+                    out.append((eng, t, lo * P, 4 * P))
+                    out.append((eng, t, 4 * P, hi * P))
+                else:
+                    out.append((eng, t, lo * P, hi * P))
+    return tuple(out)
+
+
+XHAT_SHARES = {4: share_table(4), 2: share_table(2), 1: share_table(1)}
+XHAT_SHARES_OF_LAST = tuple(("vector", t, 0, D) for t in range(GROUP_TILES[-1]))
 
 COL_BIAS = 0
 COL_GAMMA_BETA = COL_BIAS + F // P
@@ -71,18 +90,23 @@ def tile_gaublock_pb_t_kernel(
 
         tiles = {}
 
+        def rows_of(g):
+            first = sum(GROUP_TILES[:g]) * P
+            return slice(first, first + GROUP_TILES[g] * P)
+
         def live(g):
             return 0 <= g < GROUPS
 
         def shares(g):
-            return XHAT_SHARES_OF_LAST if g == GROUPS - 1 else XHAT_SHARES
+            return XHAT_SHARES_OF_LAST if g == GROUPS - 1 else XHAT_SHARES[GROUP_TILES[g]]
 
         def load(g):
-            xt = x_pool.tile([P, TILES, D], BF16, name="xt")
+            n = GROUP_TILES[g]
+            xt = x_pool.tile([P, n, D], BF16, name="xt")
             tiles[("x", g)] = xt
-            src = x_rows[g * GROUP : (g + 1) * GROUP, :].rearrange("(p t) k -> p t k", t=TILES)
+            src = x_rows[rows_of(g), :].rearrange("(p t) k -> p t k", t=n)
             if g == 0:
-                for t in range(TILES):
+                for t in range(n):
                     nc.sync.dma_start(out=xt[:, t, :], in_=src[:, t, :])
             else:
                 nc.sync.dma_start(out=xt[:], in_=src)
@@ -129,7 +153,7 @@ def tile_gaublock_pb_t_kernel(
 
         def prepare_w():
             w_words = const.tile([P, PASSES, F, PACK], BF16, align_bytes=64)
-            nc.vector.tensor_copy(out=w_words[:], in_=w_raw[:].rearrange("p c t f -> p c f t"))
+            (nc.scalar.copy if WS else nc.vector.tensor_copy)(out=w_words[:], in_=w_raw[:].rearrange("p c t f -> p c f t"))
             nc.vector.quantize_mx(
                 out=w_codes[:].bitcast(FP8X4),
                 scales=w_scales[:],
@@ -138,8 +162,9 @@ def tile_gaublock_pb_t_kernel(
 
         def stats_tile(g, t):
             if t == 0:
-                tiles[("stats", g)] = row_pool.tile([P, TILES, D // BN_MAX, 6], F32, name="stats")
-                tiles[("mean_var", g)] = row_pool.tile([P, TILES, 2], F32, name="mean_var")
+                n = GROUP_TILES[g]
+                tiles[("stats", g)] = row_pool.tile([P, n, D // BN_MAX, 6], F32, name="stats")
+                tiles[("mean_var", g)] = row_pool.tile([P, n, 2], F32, name="mean_var")
             for h in range(D // BN_MAX):
                 nc.vector.bn_stats(
                     out=tiles[("stats", g)][:, t, h, :], in_=tiles[("x", g)][:, t, h * BN_MAX : (h + 1) * BN_MAX]
@@ -153,20 +178,22 @@ def tile_gaublock_pb_t_kernel(
 
         def row_scalars(g):
             mean_var = tiles[("mean_var", g)]
-            neg_mean = row_pool.tile([P, TILES], F32, name="neg_mean")
-            var_eps = row_pool.tile([P, TILES], F32, name="var_eps")
+            neg_mean = row_pool.tile([P, GROUP_TILES[g]], F32, name="neg_mean")
+            var_eps = row_pool.tile([P, GROUP_TILES[g]], F32, name="var_eps")
             nc.vector.tensor_scalar(out=neg_mean[:], in0=mean_var[:, :, 0], scalar1=-1.0, scalar2=None, op0=ALU.mult)
             nc.vector.tensor_scalar(out=var_eps[:], in0=mean_var[:, :, 1], scalar1=LN_EPS, scalar2=None, op0=ALU.add)
             tiles[("neg_mean", g)] = neg_mean
             tiles[("var_eps", g)] = var_eps
 
         def inverse_std(g):
-            rstd = row_pool.tile([P, TILES], F32, name="rstd")
-            nc.gpsimd.tensor_tensor(out=rstd[:], in0=tiles[("var_eps", g)][:], in1=minus_half[:], op=ALU.pow)
+            rstd = row_pool.tile([P, GROUP_TILES[g]], F32, name="rstd")
+            nc.gpsimd.tensor_tensor(
+                out=rstd[:], in0=tiles[("var_eps", g)][:], in1=minus_half[:, 0 : GROUP_TILES[g]], op=ALU.pow
+            )
             tiles[("rstd", g)] = rstd
 
         def scalar_bias(g):
-            bias = row_pool.tile([P, TILES], F32, name="bias")
+            bias = row_pool.tile([P, GROUP_TILES[g]], F32, name="bias")
             nc.gpsimd.tensor_tensor(
                 out=bias[:], in0=tiles[("neg_mean", g)][:], in1=tiles[("rstd", g)][:], op=ALU.mult
             )
@@ -175,10 +202,11 @@ def tile_gaublock_pb_t_kernel(
         def xhat(g, engine):
             mine = [share[1:] for share in shares(g) if share[0] == engine]
             if mine and ("xhat", g) not in tiles:
-                tiles[("xhat", g)] = work.tile([P, TILES, D], F32, name="xhat")
+                tiles[("xhat", g)] = work.tile([P, GROUP_TILES[g], D], F32, name="xhat")
             for t, lo, hi in mine:
-                dst = tiles[("xhat", g)][:, t, lo:hi].rearrange("p (c t k) -> p c t k", t=PACK, k=P)
-                src = tiles[("x", g)][:, t, lo:hi].rearrange("p (c k t) -> p c t k", t=PACK, k=P)
+                c0, c1, t0, t1 = lo // 512, (hi + 511) // 512, (lo % 512) // P, 4 if hi % 512 == 0 else (hi % 512) // P
+                dst = tiles[("xhat", g)][:, t, :].rearrange("p (c t k) -> p c t k", t=PACK, k=P)[:, c0:c1, t0:t1]
+                src = tiles[("x", g)][:, t, :].rearrange("p (c k t) -> p c t k", t=PACK, k=P)[:, c0:c1, t0:t1]
                 rstd = tiles[("rstd", g)][:, t : t + 1]
                 if engine == "scalar":
                     nc.scalar.activation(
@@ -192,31 +220,41 @@ def tile_gaublock_pb_t_kernel(
                     )
 
         def turn(g, j):
+            n = GROUP_TILES[g]
             if j == 0:
-                tiles[("planes", g)] = work.tile([P, PASSES, PACK, GROUP], BF16, name="planes")
+                tiles[("planes", g)] = work.tile([P, PASSES, PACK, n * P], BF16, name="planes")
             bank = turn_banks.tile([P, GROUP], F32, tag="bank", name="bank")
-            for t in range(TILES):
+            for t in range(n):
                 nc.tensor.transpose(
                     out=bank[:, t * P : (t + 1) * P],
                     in_=tiles[("xhat", g)][:, t, j * P : (j + 1) * P],
                     identity=ident[:],
                 )
             nc.scalar.activation(
-                out=tiles[("planes", g)][:, j // PACK, j % PACK, :], in_=bank[:], func=ACT.Identity,
+                out=tiles[("planes", g)][:, j // PACK, j % PACK, :], in_=bank[:, 0 : n * P], func=ACT.Identity,
                 bias=offset[:, j // PACK, j % PACK : j % PACK + 1], scale=gain[:, j // PACK, j % PACK : j % PACK + 1],
             )
 
-        def regroup(g, c):
-            if c == 0:
-                tiles[("words", g)] = work.tile([P, PASSES, GROUP, PACK], BF16, align_bytes=64, name="words")
-            nc.vector.tensor_copy(
-                out=tiles[("words", g)][:, c].rearrange("p (w i) t -> p w t i", i=4),
-                in_=tiles[("planes", g)][:, c].rearrange("p t (w i) -> p w t i", i=4),
-            )
+        def regroup(g, c, engine):
+            n = GROUP_TILES[g] * P
+            cut = COPY_S * n // 512 if c == 0 else 0
+            lo, hi = (0, cut) if engine == "scalar" else (cut, n)
+            if ("words", g) not in tiles:
+                tiles[("words", g)] = work.tile(
+                    [P, PASSES, GROUP_TILES[g] * P, PACK], BF16, align_bytes=64, name="words"
+                )
+            if lo == hi:
+                return
+            dst = tiles[("words", g)][:, c, lo:hi].rearrange("p (w i) t -> p w t i", i=RUN)
+            src = tiles[("planes", g)][:, c, :, lo:hi].rearrange("p t (w i) -> p w t i", i=RUN)
+            if engine == "scalar":
+                nc.scalar.copy(out=dst, in_=src)
+            else:
+                nc.vector.tensor_copy(out=dst, in_=src)
 
         def quantise(g):
-            codes = work.tile([P, PASSES * GROUP], U32, align_bytes=64, name="codes")
-            scales = work.tile([P, PASSES * GROUP], U8, align_bytes=64, name="scales")
+            codes = work.tile([P, PASSES * GROUP_TILES[g] * P], U32, align_bytes=64, name="codes")
+            scales = work.tile([P, PASSES * GROUP_TILES[g] * P], U8, align_bytes=64, name="scales")
             nc.vector.quantize_mx(
                 out=codes[:].bitcast(FP8X4), scales=scales[:],
                 in_=tiles[("words", g)][:].rearrange("p c n t -> p (c n t)"),
@@ -227,7 +265,8 @@ def tile_gaublock_pb_t_kernel(
         def multiply(g):
             codes = tiles[("codes", g)]
             scales = tiles[("scales", g)]
-            silu = work.tile([P, F // P, GROUP], F32, name="silu")
+            n = GROUP_TILES[g] * P
+            silu = work.tile([P, F // P, n], F32, name="silu")
             tiles[("silu", g)] = silu
             accs = []
             for h in range(F // P):
@@ -236,22 +275,22 @@ def tile_gaublock_pb_t_kernel(
                 for c in range(PASSES):
                     w0 = c * F + h * P
                     nc.tensor.matmul_mx(
-                        out=acc[:],
+                        out=acc[:, 0:n],
                         lhsT=w_codes[:, w0 : w0 + P].bitcast(FP8X4),
                         lhsT_scale=w_scales[:, w0 : w0 + P],
-                        rhs=codes[:, c * GROUP : (c + 1) * GROUP].bitcast(FP8X4),
-                        rhs_scale=scales[:, c * GROUP : (c + 1) * GROUP],
+                        rhs=codes[:, c * n : (c + 1) * n].bitcast(FP8X4),
+                        rhs_scale=scales[:, c * n : (c + 1) * n],
                         start=(c == 0),
                         stop=(c == PASSES - 1),
                     )
             for h in range(F // P):
                 nc.scalar.activation(
-                    out=silu[:, h, :], in_=accs[h][:], func=ACT.Silu, bias=param(COL_BIAS + h), scale=1.0
+                    out=silu[:, h, :], in_=accs[h][:, 0:n], func=ACT.Silu, bias=param(COL_BIAS + h), scale=1.0
                 )
 
         def scale_offset(g):
             z = tiles[("silu", g)][:, 1, :]
-            qk = work.tile([P, 2, GROUP], F32, name="qk")
+            qk = work.tile([P, 2, GROUP_TILES[g] * P], F32, name="qk")
             tiles[("qk", g)] = qk
             for i in range(2):
                 nc.vector.tensor_scalar(
@@ -262,28 +301,29 @@ def tile_gaublock_pb_t_kernel(
 
         def emit_out(g, i):
             src = tiles[("silu", g)][:, 0, :] if i == 0 else tiles[("qk", g)][:, i - 1, :]
-            rows = slice(g * GROUP, (g + 1) * GROUP)
+            n = GROUP_TILES[g]
+            rows = rows_of(g)
             bank = turn_banks.tile([P, GROUP], F32, tag="bank", name="out_bank")
-            for t in range(TILES):
+            for t in range(n):
                 nc.tensor.transpose(
                     out=bank[:, t * P : (t + 1) * P], in_=src[:, t * P : (t + 1) * P], identity=ident[:]
                 )
             if i == 0:
-                uv = store_pool.tile([P, 2, TILES, E], F32, name="uv")
-                nc.scalar.copy(
+                uv = store_pool.tile([P, 2, n, E], F32, name="uv")
+                (nc.vector.tensor_copy if 0 in EXIT_V else nc.scalar.copy)(
                     out=uv[:].rearrange("p c t f -> p t c f"),
-                    in_=bank[:].rearrange("p (t c f) -> p t c f", t=TILES, c=2),
+                    in_=bank[:, 0 : n * P].rearrange("p (t c f) -> p t c f", t=n, c=2),
                 )
                 for c in range(2):
                     nc.sync.dma_start(
-                        out=outs[c][rows, :].rearrange("(p t) f -> p (t f)", t=TILES),
+                        out=outs[c][rows, :].rearrange("(p t) f -> p (t f)", t=n),
                         in_=uv[:, c].rearrange("p t f -> p (t f)"),
                     )
             else:
-                q_or_k = store_pool.tile([P, TILES * S], F32, name="q_or_k", bufs=6)
-                nc.scalar.copy(out=q_or_k[:], in_=bank[:])
+                q_or_k = store_pool.tile([P, n * S], F32, name="q_or_k", bufs=6)
+                (nc.vector.tensor_copy if i in EXIT_V else nc.scalar.copy)(out=q_or_k[:], in_=bank[:, 0 : n * P])
                 nc.sync.dma_start(
-                    out=outs[1 + i][rows, :].rearrange("(p t) f -> p (t f)", t=TILES), in_=q_or_k[:]
+                    out=outs[1 + i][rows, :].rearrange("(p t) f -> p (t f)", t=n), in_=q_or_k[:]
                 )
 
         for i in range(-STAT_AHEAD, GROUPS + 1):
@@ -295,11 +335,11 @@ def tile_gaublock_pb_t_kernel(
             if live(g_xhat - 1):
                 xhat(g_xhat - 1, "vector")
             if live(i):
-                regroup(i, 0)
+                regroup(i, 0, "vector")
             if live(g_stat - 1):
-                aggregate(g_stat - 1, TILES - 1)
+                aggregate(g_stat - 1, GROUP_TILES[g_stat - 1] - 1)
             if live(i):
-                regroup(i, 1)
+                regroup(i, 1, "vector")
             if live(i) and not live(g_stat):
                 quantise(i)
             if live(i - 1):
@@ -316,17 +356,19 @@ def tile_gaublock_pb_t_kernel(
                 xhat(g_xhat, "gpsimd")
             if live(g_stat):
                 stats_tile(g_stat, 0)
-                for t in range(1, TILES):
+                for t in range(1, GROUP_TILES[g_stat]):
                     stats_tile(g_stat, t)
                     aggregate(g_stat, t - 1)
-            if g_stat == 0:
-                prepare_params()
             if g_stat == 1:
+                prepare_params()
+            if g_stat == 2:
                 prepare_w()
 
             if live(i + 1):
                 for j in range(K_BLOCKS):
                     turn(i + 1, j)
+                    if j == 3:
+                        regroup(i + 1, 0, "scalar")
             if live(g_xhat):
                 xhat(g_xhat, "scalar")
             if live(i):

@@ -35,8 +35,8 @@ STAT_AHEAD = 3
 XHAT_AHEAD = 2
 assert XHAT_AHEAD == STAT_AHEAD - 1
 
-GS = 18
-VS = 0
+GS = 14
+VS = 6
 COPY_S = 0
 EXIT_V = ()
 WS = 1

@@ -38,9 +38,19 @@ assert XHAT_AHEAD == STAT_AHEAD - 1
 GS = 14
 VS = 6
 COPY_S = 0
-EXIT_V = ()
+EXIT_V = (2,)
 WS = 1
 RUN = 4
+WARM = ((0, 0), (0, 1), (3, 0), (3, 1))
+WARM_OUT = ((0, 0), (0, 1))
+HALVES = (1, 0)
+OUT_ORDER = (1, 2, 0)
+LP = 0
+VP = (1, 3, 5)
+LE = 0
+SSTATS_A = ()
+SSTATS_B = ()
+SSTATS = SSTATS_A + SSTATS_B
 
 
 def share_table(n):
@@ -59,7 +69,11 @@ def share_table(n):
 
 
 XHAT_SHARES = {4: share_table(4), 2: share_table(2), 1: share_table(1)}
-XHAT_SHARES_OF_LAST = tuple(("vector", t, 0, D) for t in range(GROUP_TILES[-1]))
+XL = "vvvv"
+XHAT_SHARES_OF_LAST = tuple(({"v": "vector", "g": "gpsimd", "s": "scalar"}[XL[t]], t, 0, D) for t in range(GROUP_TILES[-1]))
+CL = 0
+CLN = 2
+CL1 = 0
 
 COL_BIAS = 0
 COL_GAMMA_BETA = COL_BIAS + F // P
@@ -165,12 +179,28 @@ def tile_gaublock_pb_t_kernel(
                 n = GROUP_TILES[g]
                 tiles[("stats", g)] = row_pool.tile([P, n, D // BN_MAX, 6], F32, name="stats")
                 tiles[("mean_var", g)] = row_pool.tile([P, n, 2], F32, name="mean_var")
+            if (g, t) in SSTATS:
+                return
             for h in range(D // BN_MAX):
                 nc.vector.bn_stats(
                     out=tiles[("stats", g)][:, t, h, :], in_=tiles[("x", g)][:, t, h * BN_MAX : (h + 1) * BN_MAX]
                 )
 
+        def scalar_stats(g, t):
+            xt = tiles[("x", g)][:, t, :]
+            mean_var = tiles[("mean_var", g)]
+            unused = work.tile([P, D], BF16, name="unused")
+            sums = row_pool.tile([P, 2], F32, name="sums", bufs=8)
+            neg_mean = row_pool.tile([P, 1], F32, name="neg_mean_of_tile", bufs=8)
+            nc.scalar.activation(out=unused[:], in_=xt, func=ACT.Copy, accum_out=sums[:, 0:1])
+            nc.scalar.activation(out=neg_mean[:], in_=sums[:, 0:1], func=ACT.Copy, scale=-1.0 / D)
+            nc.scalar.activation(out=unused[:], in_=xt, func=ACT.Square, bias=neg_mean[:], accum_out=sums[:, 1:2])
+            nc.scalar.activation(out=mean_var[:, t, 0:1], in_=sums[:, 0:1], func=ACT.Copy, scale=1.0 / D)
+            nc.scalar.activation(out=mean_var[:, t, 1:2], in_=sums[:, 1:2], func=ACT.Copy, scale=1.0 / D)
+
         def aggregate(g, t):
+            if (g, t) in SSTATS:
+                return
             nc.vector.bn_aggr(
                 out=tiles[("mean_var", g)][:, t, :],
                 in_=tiles[("stats", g)][:, t, :, :].rearrange("p h s -> p (h s)"),
@@ -225,19 +255,30 @@ def tile_gaublock_pb_t_kernel(
                 tiles[("planes", g)] = work.tile([P, PASSES, PACK, n * P], BF16, name="planes")
             bank = turn_banks.tile([P, GROUP], F32, tag="bank", name="bank")
             for t in range(n):
-                nc.tensor.transpose(
-                    out=bank[:, t * P : (t + 1) * P],
-                    in_=tiles[("xhat", g)][:, t, j * P : (j + 1) * P],
-                    identity=ident[:],
+                turned = bank[:, t * P : (t + 1) * P]
+                block = tiles[("xhat", g)][:, t, j * P : (j + 1) * P]
+                if (j, t) in WARM:
+                    nc.tensor.matmul(out=turned, lhsT=block, rhs=ident[:], start=True, stop=True)
+                else:
+                    nc.tensor.transpose(out=turned, in_=block, identity=ident[:])
+            if g >= GROUPS - LP and j in VP:
+                nc.vector.tensor_scalar(
+                    out=tiles[("planes", g)][:, j // PACK, j % PACK, :], in0=bank[:, 0 : n * P],
+                    scalar1=gain[:, j // PACK, j % PACK : j % PACK + 1],
+                    scalar2=offset[:, j // PACK, j % PACK : j % PACK + 1], op0=ALU.mult, op1=ALU.add,
                 )
-            nc.scalar.activation(
-                out=tiles[("planes", g)][:, j // PACK, j % PACK, :], in_=bank[:, 0 : n * P], func=ACT.Identity,
-                bias=offset[:, j // PACK, j % PACK : j % PACK + 1], scale=gain[:, j // PACK, j % PACK : j % PACK + 1],
-            )
+            else:
+                nc.scalar.activation(
+                    out=tiles[("planes", g)][:, j // PACK, j % PACK, :], in_=bank[:, 0 : n * P], func=ACT.Identity,
+                    bias=offset[:, j // PACK, j % PACK : j % PACK + 1],
+                    scale=gain[:, j // PACK, j % PACK : j % PACK + 1],
+                )
 
         def regroup(g, c, engine):
             n = GROUP_TILES[g] * P
             cut = COPY_S * n // 512 if c == 0 else 0
+            if g >= GROUPS - CLN:
+                cut = CL if c == 0 else CL1
             lo, hi = (0, cut) if engine == "scalar" else (cut, n)
             if ("words", g) not in tiles:
                 tiles[("words", g)] = work.tile(
@@ -268,10 +309,10 @@ def tile_gaublock_pb_t_kernel(
             n = GROUP_TILES[g] * P
             silu = work.tile([P, F // P, n], F32, name="silu")
             tiles[("silu", g)] = silu
-            accs = []
-            for h in range(F // P):
+            accs = {}
+            for h in HALVES:
                 acc = mx_banks.tile([P, GROUP], F32, name="acc")
-                accs.append(acc)
+                accs[h] = acc
                 for c in range(PASSES):
                     w0 = c * F + h * P
                     nc.tensor.matmul_mx(
@@ -283,7 +324,7 @@ def tile_gaublock_pb_t_kernel(
                         start=(c == 0),
                         stop=(c == PASSES - 1),
                     )
-            for h in range(F // P):
+            for h in HALVES:
                 nc.scalar.activation(
                     out=silu[:, h, :], in_=accs[h][:, 0:n], func=ACT.Silu, bias=param(COL_BIAS + h), scale=1.0
                 )
@@ -305,12 +346,15 @@ def tile_gaublock_pb_t_kernel(
             rows = rows_of(g)
             bank = turn_banks.tile([P, GROUP], F32, tag="bank", name="out_bank")
             for t in range(n):
-                nc.tensor.transpose(
-                    out=bank[:, t * P : (t + 1) * P], in_=src[:, t * P : (t + 1) * P], identity=ident[:]
-                )
+                turned = bank[:, t * P : (t + 1) * P]
+                block = src[:, t * P : (t + 1) * P]
+                if (i, t) in WARM_OUT:
+                    nc.tensor.matmul(out=turned, lhsT=block, rhs=ident[:], start=True, stop=True)
+                else:
+                    nc.tensor.transpose(out=turned, in_=block, identity=ident[:])
             if i == 0:
                 uv = store_pool.tile([P, 2, n, E], F32, name="uv")
-                (nc.vector.tensor_copy if 0 in EXIT_V else nc.scalar.copy)(
+                (nc.vector.tensor_copy if g >= GROUPS - LE and 0 in EXIT_V else nc.scalar.copy)(
                     out=uv[:].rearrange("p c t f -> p t c f"),
                     in_=bank[:, 0 : n * P].rearrange("p (t c f) -> p t c f", t=n, c=2),
                 )
@@ -321,7 +365,7 @@ def tile_gaublock_pb_t_kernel(
                     )
             else:
                 q_or_k = store_pool.tile([P, n * S], F32, name="q_or_k", bufs=6)
-                (nc.vector.tensor_copy if i in EXIT_V else nc.scalar.copy)(out=q_or_k[:], in_=bank[:, 0 : n * P])
+                (nc.vector.tensor_copy if g >= GROUPS - LE and i in EXIT_V else nc.scalar.copy)(out=q_or_k[:], in_=bank[:, 0 : n * P])
                 nc.sync.dma_start(
                     out=outs[1 + i][rows, :].rearrange("(p t) f -> p (t f)", t=n), in_=q_or_k[:]
                 )
@@ -356,6 +400,9 @@ def tile_gaublock_pb_t_kernel(
                 xhat(g_xhat, "gpsimd")
             if live(g_stat):
                 stats_tile(g_stat, 0)
+                for g, t in SSTATS_A:
+                    if g == g_stat:
+                        scalar_stats(g, t)
                 for t in range(1, GROUP_TILES[g_stat]):
                     stats_tile(g_stat, t)
                     aggregate(g_stat, t - 1)
@@ -369,10 +416,16 @@ def tile_gaublock_pb_t_kernel(
                     turn(i + 1, j)
                     if j == 3:
                         regroup(i + 1, 0, "scalar")
+                    if j == 7:
+                        regroup(i + 1, 1, "scalar")
             if live(g_xhat):
                 xhat(g_xhat, "scalar")
+            if live(g_stat):
+                for g, t in SSTATS_B:
+                    if g == g_stat:
+                        scalar_stats(g, t)
             if live(i):
                 multiply(i)
             if live(i - 1):
-                for k in range(3):
+                for k in OUT_ORDER:
                     emit_out(i - 1, k)

@@ -41,14 +41,15 @@ COPY_S = 0
 EXIT_V = (2,)
 WS = 1
 RUN = 4
+QHALF = 1
 WARM = ((0, 0), (0, 1), (3, 0), (3, 1))
 WARM_OUT = ((0, 0), (0, 1))
 HALVES = (1, 0)
 OUT_ORDER = (1, 2, 0)
 LP = 0
 VP = (1, 3, 5)
-LE = 0
-SSTATS_A = ()
+LE = 1
+SSTATS_A = ((0, 3), (1, 3))
 SSTATS_B = ()
 SSTATS = SSTATS_A + SSTATS_B
 
@@ -130,6 +131,8 @@ def tile_gaublock_pb_t_kernel(
         make_identity(nc, ident[:])
         minus_half = const.tile([P, TILES], F32)
         nc.vector.memset(minus_half[:], -0.5)
+        silu_first = const.tile([P, 1], F32)
+        nc.scalar.activation(out=silu_first[:], in_=minus_half[:, 0:1], func=ACT.Silu)
         param_rows = const.tile([P, P], BF16)
         nc.vector.memset(param_rows[:], 0.0)
         row = 0
@@ -293,15 +296,16 @@ def tile_gaublock_pb_t_kernel(
             else:
                 nc.vector.tensor_copy(out=dst, in_=src)
 
-        def quantise(g):
-            codes = work.tile([P, PASSES * GROUP_TILES[g] * P], U32, align_bytes=64, name="codes")
-            scales = work.tile([P, PASSES * GROUP_TILES[g] * P], U8, align_bytes=64, name="scales")
+        def quantise(g, first=0, end=PASSES):
+            n = GROUP_TILES[g] * P
+            if first == 0:
+                tiles[("codes", g)] = work.tile([P, PASSES * n], U32, align_bytes=64, name="codes")
+                tiles[("scales", g)] = work.tile([P, PASSES * n], U8, align_bytes=64, name="scales")
             nc.vector.quantize_mx(
-                out=codes[:].bitcast(FP8X4), scales=scales[:],
-                in_=tiles[("words", g)][:].rearrange("p c n t -> p (c n t)"),
+                out=tiles[("codes", g)][:, first * n : end * n].bitcast(FP8X4),
+                scales=tiles[("scales", g)][:, first * n : end * n],
+                in_=tiles[("words", g)][:, first:end].rearrange("p c n t -> p (c n t)"),
             )
-            tiles[("codes", g)] = codes
-            tiles[("scales", g)] = scales
 
         def multiply(g):
             codes = tiles[("codes", g)]
@@ -376,15 +380,23 @@ def tile_gaublock_pb_t_kernel(
             if i >= 0 and live(i + LOAD_AHEAD):
                 load(i + LOAD_AHEAD)
 
-            if live(g_xhat - 1):
+            last_xhat = g_xhat - 1 == GROUPS - 1
+            if live(g_xhat - 1) and not last_xhat:
                 xhat(g_xhat - 1, "vector")
             if live(i):
                 regroup(i, 0, "vector")
+            if last_xhat:
+                xhat(g_xhat - 1, "vector")
             if live(g_stat - 1):
                 aggregate(g_stat - 1, GROUP_TILES[g_stat - 1] - 1)
+            halves = live(i) and i >= GROUPS - QHALF
+            if halves:
+                quantise(i, 0, 1)
             if live(i):
                 regroup(i, 1, "vector")
-            if live(i) and not live(g_stat):
+            if halves:
+                quantise(i, 1, 2)
+            elif live(i) and not live(g_stat):
                 quantise(i)
             if live(i - 1):
                 scale_offset(i - 1)

from contextlib import ExitStack

import concourse.mybir as mybir
from concourse.masks import make_identity

F32 = mybir.dt.float32
BF16 = mybir.dt.bfloat16
U32 = mybir.dt.uint32
U8 = mybir.dt.uint8
FP8X4 = mybir.dt.float8_e4m3fn_x4
ACT = mybir.ActivationFunctionType
ALU = mybir.AluOpType

P = 128
ROWS = 8 * 1024
D = 1024
F = 256
E = 64
S = 128
LN_EPS = 1e-5
PACK = 4
K_PASS = P * PACK
PASSES = D // K_PASS
K_BLOCKS = D // P
TILES = 4
GROUP = TILES * P
GROUP_TILES = (4,) * 16
GROUPS = len(GROUP_TILES)
assert sum(GROUP_TILES) * P == ROWS
BN_MAX = 512
FLOPS = 2 * ROWS * D * F

LOAD_AHEAD = 4
STAT_AHEAD = 3
XHAT_AHEAD = 2
assert XHAT_AHEAD == STAT_AHEAD - 1

GS = 14
VS = 6
COPY_S = 0
EXIT_V = (2,)
WS = 1
RUN = 4
QHALF = 1
WARM = ((0, 0), (0, 1), (3, 0), (3, 1))
WARM_OUT = ((0, 0), (0, 1))
HALVES = (1, 0)
OUT_ORDER = (1, 2, 0)
LP = 0
VP = (1, 3, 5)
LE = 1
SSTATS_A = ((0, 3), (1, 3))
SSTATS_B = ()
SSTATS = SSTATS_A + SSTATS_B


def share_table(n):
    g, v = GS * n // 4, VS * n // 4
    out = []
    for t in range(n):
        a, b, e = min(max(g - 8 * t, 0), 8), min(max(g + v - 8 * t, 0), 8), 8
        for eng, lo, hi in (("gpsimd", 0, a), ("vector", a, b), ("scalar", b, e)):
            if hi > lo:
                if lo < 4 < hi and (lo, hi) != (0, 8):
                    out.append((eng, t, lo * P, 4 * P))
                    out.append((eng, t, 4 * P, hi * P))
                else:
                    out.append((eng, t, lo * P, hi * P))
    return tuple(out)


XHAT_SHARES = {4: share_table(4), 2: share_table(2), 1: share_table(1)}
XL = "vvvv"
XHAT_SHARES_OF_LAST = tuple(({"v": "vector", "g": "gpsimd", "s": "scalar"}[XL[t]], t, 0, D) for t in range(GROUP_TILES[-1]))
CL = 0
CLN = 2
CL1 = 0

COL_BIAS = 0
COL_GAMMA_BETA = COL_BIAS + F // P
PARAM_COLS = 32


def tile_gaublock_pb_t_kernel(
    tc, x, ln_g, ln_b, W_in, b_in, gamma_q, beta_q, gamma_k, beta_k, out_0, out_1, out_2, out_3
):
    nc = tc.nc
    x_rows = x.flatten_outer_dims()
    outs = (
        out_0.flatten_outer_dims(),
        out_1.flatten_outer_dims(),
        out_2.flatten_outer_dims(),
        out_3.flatten_outer_dims(),
    )

    with ExitStack() as ctx:
        const = ctx.enter_context(tc.tile_pool(name="const", bufs=1))
        x_pool = ctx.enter_context(tc.tile_pool(name="x_pool", bufs=LOAD_AHEAD + 1))
        row_pool = ctx.enter_context(tc.tile_pool(name="row_pool", bufs=STAT_AHEAD + 2))
        work = ctx.enter_context(tc.tile_pool(name="work", bufs=2))
        store_pool = ctx.enter_context(tc.tile_pool(name="store_pool", bufs=3))
        turn_banks = ctx.enter_context(tc.psum_pool(name="turn_banks", bufs=6))
        mx_banks = ctx.enter_context(tc.psum_pool(name="mx_banks", bufs=2))
        ctx.enter_context(tc.manual_schedule())

        tiles = {}

        def rows_of(g):
            first = sum(GROUP_TILES[:g]) * P
            return slice(first, first + GROUP_TILES[g] * P)

        def live(g):
            return 0 <= g < GROUPS

        def shares(g):
            return XHAT_SHARES_OF_LAST if g == GROUPS - 1 else XHAT_SHARES[GROUP_TILES[g]]

        def load(g):
            n = GROUP_TILES[g]
            xt = x_pool.tile([P, n, D], BF16, name="xt")
            tiles[("x", g)] = xt
            src = x_rows[rows_of(g), :].rearrange("(p t) k -> p t k", t=n)
            if g == 0:
                for t in range(n):
                    nc.sync.dma_start(out=xt[:, t, :], in_=src[:, t, :])
            else:
                nc.sync.dma_start(out=xt[:], in_=src)

        load(0)
        ident = const.tile([P, P], F32)
        make_identity(nc, ident[:])
        minus_half = const.tile([P, TILES], F32)
        nc.vector.memset(minus_half[:], -0.5)
        silu_first = const.tile([P, 1], F32)
        nc.scalar.activation(out=silu_first[:], in_=minus_half[:, 0:1], func=ACT.Silu)
        param_rows = const.tile([P, P], BF16)
        nc.vector.memset(param_rows[:], 0.0)
        row = 0
        gain_bf16 = const.tile([P, PASSES, PACK], BF16)
        offset_bf16 = const.tile([P, PASSES, PACK], BF16)
        for dst, vec in ((gain_bf16, ln_g), (offset_bf16, ln_b)):
            nc.scalar.dma_start(out=dst[:], in_=vec.rearrange("(c p t) -> p c t", p=P, t=PACK))
        for vec in (b_in, gamma_q, beta_q, gamma_k, beta_k):
            n = vec.shape[0] // P
            nc.scalar.dma_start(out=param_rows[row : row + n, :], in_=vec.rearrange("(j p) -> j p", p=P))
            row += n
        load(1)
        w_raw = const.tile([P, PASSES, PACK, F], BF16)
        nc.sync.dma_start(out=w_raw[:], in_=W_in.rearrange("(c p t) f -> p c t f", p=P, t=PACK))
        for g in range(2, LOAD_AHEAD):
            load(g)

        gain = const.tile([P, PASSES, PACK], F32)
        offset = const.tile([P, PASSES, PACK], F32)
        params = const.tile([P, PARAM_COLS], F32)
        w_codes = const.tile([P, PASSES * F], U32, align_bytes=64)
        w_scales = const.tile([P, PASSES * F], U8, align_bytes=64)

        def param(col):
            return params[:, col : col + 1]

        def prepare_params():
            nc.vector.tensor_copy(out=gain[:], in_=gain_bf16[:])
            nc.vector.tensor_copy(out=offset[:], in_=offset_bf16[:])
            param_f32 = const.tile([P, P], F32)
            nc.vector.tensor_copy(out=param_f32[:], in_=param_rows[:])
            bank = turn_banks.tile([P, GROUP], F32, tag="bank", name="param_bank")
            nc.tensor.transpose(out=bank[:, 0:P], in_=param_f32[:], identity=ident[:])
            nc.vector.tensor_copy(out=params[:], in_=bank[:, 0:PARAM_COLS])

        def prepare_w():
            w_words = const.tile([P, PASSES, F, PACK], BF16, align_bytes=64)
            (nc.scalar.copy if WS else nc.vector.tensor_copy)(out=w_words[:], in_=w_raw[:].rearrange("p c t f -> p c f t"))
            nc.vector.quantize_mx(
                out=w_codes[:].bitcast(FP8X4),
                scales=w_scales[:],
                in_=w_words[:].rearrange("p c f t -> p (c f t)"),
            )

        def stats_tile(g, t):
            if t == 0:
                n = GROUP_TILES[g]
                tiles[("stats", g)] = row_pool.tile([P, n, D // BN_MAX, 6], F32, name="stats")
                tiles[("mean_var", g)] = row_pool.tile([P, n, 2], F32, name="mean_var")
            if (g, t) in SSTATS:
                return
            for h in range(D // BN_MAX):
                nc.vector.bn_stats(
                    out=tiles[("stats", g)][:, t, h, :], in_=tiles[("x", g)][:, t, h * BN_MAX : (h + 1) * BN_MAX]
                )

        def scalar_stats(g, t):
            xt = tiles[("x", g)][:, t, :]
            mean_var = tiles[("mean_var", g)]
            unused = work.tile([P, D], BF16, name="unused")
            sums = row_pool.tile([P, 2], F32, name="sums", bufs=8)
            neg_mean = row_pool.tile([P, 1], F32, name="neg_mean_of_tile", bufs=8)
            nc.scalar.activation(out=unused[:], in_=xt, func=ACT.Copy, accum_out=sums[:, 0:1])
            nc.scalar.activation(out=neg_mean[:], in_=sums[:, 0:1], func=ACT.Copy, scale=-1.0 / D)
            nc.scalar.activation(out=unused[:], in_=xt, func=ACT.Square, bias=neg_mean[:], accum_out=sums[:, 1:2])
            nc.scalar.activation(out=mean_var[:, t, 0:1], in_=sums[:, 0:1], func=ACT.Copy, scale=1.0 / D)
            nc.scalar.activation(out=mean_var[:, t, 1:2], in_=sums[:, 1:2], func=ACT.Copy, scale=1.0 / D)

        def aggregate(g, t):
            if (g, t) in SSTATS:
                return
            nc.vector.bn_aggr(
                out=tiles[("mean_var", g)][:, t, :],
                in_=tiles[("stats", g)][:, t, :, :].rearrange("p h s -> p (h s)"),
            )

        def row_scalars(g):
            mean_var = tiles[("mean_var", g)]
            neg_mean = row_pool.tile([P, GROUP_TILES[g]], F32, name="neg_mean")
            var_eps = row_pool.tile([P, GROUP_TILES[g]], F32, name="var_eps")
            nc.vector.tensor_scalar(out=neg_mean[:], in0=mean_var[:, :, 0], scalar1=-1.0, scalar2=None, op0=ALU.mult)
            nc.vector.tensor_scalar(out=var_eps[:], in0=mean_var[:, :, 1], scalar1=LN_EPS, scalar2=None, op0=ALU.add)
            tiles[("neg_mean", g)] = neg_mean
            tiles[("var_eps", g)] = var_eps

        def inverse_std(g):
            rstd = row_pool.tile([P, GROUP_TILES[g]], F32, name="rstd")
            nc.gpsimd.tensor_tensor(
                out=rstd[:], in0=tiles[("var_eps", g)][:], in1=minus_half[:, 0 : GROUP_TILES[g]], op=ALU.pow
            )
            tiles[("rstd", g)] = rstd

        def scalar_bias(g):
            bias = row_pool.tile([P, GROUP_TILES[g]], F32, name="bias")
            nc.gpsimd.tensor_tensor(
                out=bias[:], in0=tiles[("neg_mean", g)][:], in1=tiles[("rstd", g)][:], op=ALU.mult
            )
            tiles[("bias", g)] = bias

        def xhat(g, engine):
            mine = [share[1:] for share in shares(g) if share[0] == engine]
            if mine and ("xhat", g) not in tiles:
                tiles[("xhat", g)] = work.tile([P, GROUP_TILES[g], D], F32, name="xhat")
            for t, lo, hi in mine:
                c0, c1, t0, t1 = lo // 512, (hi + 511) // 512, (lo % 512) // P, 4 if hi % 512 == 0 else (hi % 512) // P
                dst = tiles[("xhat", g)][:, t, :].rearrange("p (c t k) -> p c t k", t=PACK, k=P)[:, c0:c1, t0:t1]
                src = tiles[("x", g)][:, t, :].rearrange("p (c k t) -> p c t k", t=PACK, k=P)[:, c0:c1, t0:t1]
                rstd = tiles[("rstd", g)][:, t : t + 1]
                if engine == "scalar":
                    nc.scalar.activation(
                        out=dst, in_=src, func=ACT.Identity, bias=tiles[("bias", g)][:, t : t + 1], scale=rstd
                    )
                else:
                    eng = nc.gpsimd if engine == "gpsimd" else nc.vector
                    eng.tensor_scalar(
                        out=dst, in0=src, scalar1=tiles[("neg_mean", g)][:, t : t + 1], scalar2=rstd,
                        op0=ALU.add, op1=ALU.mult,
                    )

        def turn(g, j):
            n = GROUP_TILES[g]
            if j == 0:
                tiles[("planes", g)] = work.tile([P, PASSES, PACK, n * P], BF16, name="planes")
            bank = turn_banks.tile([P, GROUP], F32, tag="bank", name="bank")
            for t in range(n):
                turned = bank[:, t * P : (t + 1) * P]
                block = tiles[("xhat", g)][:, t, j * P : (j + 1) * P]
                if (j, t) in WARM:
                    nc.tensor.matmul(out=turned, lhsT=block, rhs=ident[:], start=True, stop=True)
                else:
                    nc.tensor.transpose(out=turned, in_=block, identity=ident[:])
            if g >= GROUPS - LP and j in VP:
                nc.vector.tensor_scalar(
                    out=tiles[("planes", g)][:, j // PACK, j % PACK, :], in0=bank[:, 0 : n * P],
                    scalar1=gain[:, j // PACK, j % PACK : j % PACK + 1],
                    scalar2=offset[:, j // PACK, j % PACK : j % PACK + 1], op0=ALU.mult, op1=ALU.add,
                )
            else:
                nc.scalar.activation(
                    out=tiles[("planes", g)][:, j // PACK, j % PACK, :], in_=bank[:, 0 : n * P], func=ACT.Identity,
                    bias=offset[:, j // PACK, j % PACK : j % PACK + 1],
                    scale=gain[:, j // PACK, j % PACK : j % PACK + 1],
                )

        def regroup(g, c, engine):
            n = GROUP_TILES[g] * P
            cut = COPY_S * n // 512 if c == 0 else 0
            if g >= GROUPS - CLN:
                cut = CL if c == 0 else CL1
            lo, hi = (0, cut) if engine == "scalar" else (cut, n)
            if ("words", g) not in tiles:
                tiles[("words", g)] = work.tile(
                    [P, PASSES, GROUP_TILES[g] * P, PACK], BF16, align_bytes=64, name="words"
                )
            if lo == hi:
                return
            dst = tiles[("words", g)][:, c, lo:hi].rearrange("p (w i) t -> p w t i", i=RUN)
            src = tiles[("planes", g)][:, c, :, lo:hi].rearrange("p t (w i) -> p w t i", i=RUN)
            if engine == "scalar":
                nc.scalar.copy(out=dst, in_=src)
            else:
                nc.vector.tensor_copy(out=dst, in_=src)

        def quantise(g, first=0, end=PASSES):
            n = GROUP_TILES[g] * P
            if first == 0:
                tiles[("codes", g)] = work.tile([P, PASSES * n], U32, align_bytes=64, name="codes")
                tiles[("scales", g)] = work.tile([P, PASSES * n], U8, align_bytes=64, name="scales")
            nc.vector.quantize_mx(
                out=tiles[("codes", g)][:, first * n : end * n].bitcast(FP8X4),
                scales=tiles[("scales", g)][:, first * n : end * n],
                in_=tiles[("words", g)][:, first:end].rearrange("p c n t -> p (c n t)"),
            )

        def multiply(g):
            codes = tiles[("codes", g)]
            scales = tiles[("scales", g)]
            n = GROUP_TILES[g] * P
            silu = work.tile([P, F // P, n], F32, name="silu")
            tiles[("silu", g)] = silu
            accs = {}
            for h in HALVES:
                acc = mx_banks.tile([P, GROUP], F32, name="acc")
                accs[h] = acc
                for c in range(PASSES):
                    w0 = c * F + h * P
                    nc.tensor.matmul_mx(
                        out=acc[:, 0:n],
                        lhsT=w_codes[:, w0 : w0 + P].bitcast(FP8X4),
                        lhsT_scale=w_scales[:, w0 : w0 + P],
                        rhs=codes[:, c * n : (c + 1) * n].bitcast(FP8X4),
                        rhs_scale=scales[:, c * n : (c + 1) * n],
                        start=(c == 0),
                        stop=(c == PASSES - 1),
                    )
            for h in HALVES:
                nc.scalar.activation(
                    out=silu[:, h, :], in_=accs[h][:, 0:n], func=ACT.Silu, bias=param(COL_BIAS + h), scale=1.0
                )

        def scale_offset(g):
            z = tiles[("silu", g)][:, 1, :]
            qk = work.tile([P, 2, GROUP_TILES[g] * P], F32, name="qk")
            tiles[("qk", g)] = qk
            for i in range(2):
                nc.vector.tensor_scalar(
                    out=qk[:, i, :], in0=z,
                    scalar1=param(COL_GAMMA_BETA + 2 * i), scalar2=param(COL_GAMMA_BETA + 2 * i + 1),
                    op0=ALU.mult, op1=ALU.add,
                )

        def emit_out(g, i):
            src = tiles[("silu", g)][:, 0, :] if i == 0 else tiles[("qk", g)][:, i - 1, :]
            n = GROUP_TILES[g]
            rows = rows_of(g)
            bank = turn_banks.tile([P, GROUP], F32, tag="bank", name="out_bank")
            for t in range(n):
                turned = bank[:, t * P : (t + 1) * P]
                block = src[:, t * P : (t + 1) * P]
                if (i, t) in WARM_OUT:
                    nc.tensor.matmul(out=turned, lhsT=block, rhs=ident[:], start=True, stop=True)
                else:
                    nc.tensor.transpose(out=turned, in_=block, identity=ident[:])
            if i == 0:
                uv = store_pool.tile([P, 2, n, E], F32, name="uv")
                (nc.vector.tensor_copy if g >= GROUPS - LE and 0 in EXIT_V else nc.scalar.copy)(
                    out=uv[:].rearrange("p c t f -> p t c f"),
                    in_=bank[:, 0 : n * P].rearrange("p (t c f) -> p t c f", t=n, c=2),
                )
                for c in range(2):
                    nc.sync.dma_start(
                        out=outs[c][rows, :].rearrange("(p t) f -> p (t f)", t=n),
                        in_=uv[:, c].rearrange("p t f -> p (t f)"),
                    )
            else:
                q_or_k = store_pool.tile([P, n * S], F32, name="q_or_k", bufs=6)
                (nc.vector.tensor_copy if g >= GROUPS - LE and i in EXIT_V else nc.scalar.copy)(out=q_or_k[:], in_=bank[:, 0 : n * P])
                nc.sync.dma_start(
                    out=outs[1 + i][rows, :].rearrange("(p t) f -> p (t f)", t=n), in_=q_or_k[:]
                )

        for i in range(-STAT_AHEAD, GROUPS + 1):
            g_stat = i + STAT_AHEAD
            g_xhat = i + XHAT_AHEAD
            if i >= 0 and live(i + LOAD_AHEAD):
                load(i + LOAD_AHEAD)

            last_xhat = g_xhat - 1 == GROUPS - 1
            if live(g_xhat - 1) and not last_xhat:
                xhat(g_xhat - 1, "vector")
            if live(i):
                regroup(i, 0, "vector")
            if last_xhat:
                xhat(g_xhat - 1, "vector")
            if live(g_stat - 1):
                aggregate(g_stat - 1, GROUP_TILES[g_stat - 1] - 1)
            halves = live(i) and i >= GROUPS - QHALF
            if halves:
                quantise(i, 0, 1)
            if live(i):
                regroup(i, 1, "vector")
            if halves:
                quantise(i, 1, 2)
            elif live(i) and not live(g_stat):
                quantise(i)
            if live(i - 1):
                scale_offset(i - 1)
            if live(g_stat - 1):
                row_scalars(g_stat - 1)
            if live(i) and live(g_stat):
                quantise(i)

            if live(g_xhat):
                inverse_std(g_xhat)
                if any(share[0] == "scalar" for share in shares(g_xhat)):
                    scalar_bias(g_xhat)
                xhat(g_xhat, "gpsimd")
            if live(g_stat):
                stats_tile(g_stat, 0)
                for g, t in SSTATS_A:
                    if g == g_stat:
                        scalar_stats(g, t)
                for t in range(1, GROUP_TILES[g_stat]):
                    stats_tile(g_stat, t)
                    aggregate(g_stat, t - 1)
            if g_stat == 1:
                prepare_params()
            if g_stat == 2:
                prepare_w()

            if live(i + 1):
                for j in range(K_BLOCKS):
                    turn(i + 1, j)
                    if j == 3:
                        regroup(i + 1, 0, "scalar")
                    if j == 7:
                        regroup(i + 1, 1, "scalar")
            if live(g_xhat):
                xhat(g_xhat, "scalar")
            if live(g_stat):
                for g, t in SSTATS_B:
                    if g == g_stat:
                        scalar_stats(g, t)
            if live(i):
                multiply(i)
            if live(i - 1):
                for k in OUT_ORDER:
                    emit_out(i - 1, k)
